import numpy as np
import ml_dtypes


def mxq(x, axis, fmt="e4m3"):
    dtype, down = {"e4m3": (ml_dtypes.float8_e4m3fn, 7), "e5m2": (ml_dtypes.float8_e5m2, 14)}[fmt]
    v = np.moveaxis(np.asarray(x, np.float32).astype(ml_dtypes.bfloat16).astype(np.float64), axis, -1)
    blocks = v.reshape(v.shape[:-1] + (-1, 32))
    amax = np.abs(blocks).max(-1, keepdims=True)
    byte = np.maximum(np.where(amax > 0, np.frexp(amax)[1] - 1 + 127, 0) - down, 1)
    scale = np.exp2(byte - 127.0)
    codes = (blocks / scale).astype(np.float32).astype(dtype).astype(np.float64)
    return np.moveaxis((codes * scale).reshape(v.shape), -1, axis)


WIDE = False


def mx_kscale(k):
    if not WIDE:
        return np.ones(k)
    levels = np.array([20, -20, 10, -10, 0])
    a = np.random.permutation(np.resize(levels, k // 512 * 4)).reshape(k // 512, 4)
    idx = np.arange(k)
    return np.exp2(a[idx // 512, idx % 128 // 32])


BF16 = ml_dtypes.bfloat16


def bf(x):
    return np.asarray(x, np.float32).astype(BF16)


def f64(x):
    return np.asarray(x).astype(np.float64)


M, K, N = 8192, 512, 512


def setup_inputs():
    s = mx_kscale(M)[:, None]
    A = np.random.standard_normal((M, K)) * s
    B = np.random.standard_normal((K, N)) * 2.0 / np.sqrt(K)
    g = np.random.standard_normal((M, N)) * np.exp2(np.random.randint(-12, 1, (M, 1))) * 0.25 / s
    return {"A": bf(A), "B": bf(B), "grad_out": bf(g)}


def reference(A, B, grad_out):
    a = mxq(np.tril(f64(A)), 0, "e4m3")
    g = mxq(np.tril(f64(grad_out)), 0, "e5m2")
    return np.tril(a.T @ g)

@@ -1,0 +1,139 @@
+from contextlib import ExitStack
+
+import concourse.mybir as mybir
+
+BF16 = mybir.dt.bfloat16
+F32 = mybir.dt.float32
+U32 = mybir.dt.uint32
+U8 = mybir.dt.uint8
+E4M3X4 = mybir.dt.float8_e4m3fn_x4
+E5M2X4 = mybir.dt.float8_e5m2_x4
+ALU = mybir.AluOpType
+
+P = 128
+PACK = 4
+K_PASS = P * PACK
+ROWS = 8192
+COLS = 512
+PASSES = ROWS // K_PASS
+M_TILES = COLS // P
+WIDE = PACK * COLS
+
+FLOPS = 2 * ROWS * COLS * COLS
+BYTES = 2 * ROWS * COLS * 2 + COLS * COLS * 4
+
+PASS_ORDER = [1, 2, 0] + list(range(3, PASSES))
+
+
+def regroup_views(dst, src):
+    return (
+        dst.rearrange("p (c i t) -> p c t i", i=4, t=PACK),
+        src.rearrange("p (t c i) -> p c t i", t=PACK, i=4),
+    )
+
+
+def tile_modelnew_t_kernel(tc, A, B, grad_out, out):
+    nc = tc.nc
+    a_rows = A.rearrange("(c p j) w -> c p (j w)", p=P, j=PACK)
+    g_rows = grad_out.rearrange("(c p j) w -> c p (j w)", p=P, j=PACK)
+    out_rows = out.rearrange("(m p) n -> m p n", p=P)
+
+    with ExitStack() as ctx:
+        const = ctx.enter_context(tc.tile_pool(name="const", bufs=1))
+        raw = ctx.enter_context(tc.tile_pool(name="raw", bufs=PASSES))
+        grp = ctx.enter_context(tc.tile_pool(name="grp", bufs=3))
+        mx = ctx.enter_context(tc.tile_pool(name="mx", bufs=3))
+        psum = ctx.enter_context(tc.psum_pool(name="psum", bufs=1))
+        ctx.enter_context(tc.manual_schedule())
+
+        a_raw = {}
+        g_raw = {}
+        for c in PASS_ORDER:
+            a_raw[c] = raw.tile([P, WIDE], BF16, tag="a_raw", name="a_raw%d" % c)
+            nc.sync.dma_start(out=a_raw[c][:], in_=a_rows[c])
+            g_raw[c] = raw.tile([P, WIDE], BF16, tag="g_raw", name="g_raw%d" % c)
+            nc.sync.dma_start(out=g_raw[c][:], in_=g_rows[c])
+
+        in_mask = const.tile([P, WIDE], F32, name="in_mask")
+        out_mask = const.tile([P, COLS], F32, name="out_mask")
+        out_sb = const.tile([P, M_TILES, COLS], F32, name="out_sb")
+        nc.vector.memset(in_mask[:], 1.0)
+        nc.vector.memset(out_mask[:], 1.0)
+        nc.vector.memset(out_sb[:], 0.0)
+        in_mask_wt = in_mask[:].rearrange("p (w t) -> p w t", t=PACK)
+        nc.gpsimd.affine_select(
+            out=in_mask_wt,
+            in_=in_mask_wt,
+            pattern=[[-1, COLS], [1, PACK]],
+            compare_op=ALU.is_ge,
+            fill=0.0,
+            base=0,
+            channel_multiplier=PACK,
+        )
+        nc.gpsimd.affine_select(
+            out=out_mask[:],
+            in_=out_mask[:],
+            pattern=[[-1, COLS]],
+            compare_op=ALU.is_ge,
+            fill=0.0,
+            base=COLS - P,
+            channel_multiplier=1,
+        )
+
+        acc = [psum.tile([P, COLS], F32, name="acc%d" % m) for m in range(M_TILES)]
+
+        grouped = {}
+
+        def regroup(c):
+            a_grp = grp.tile([P, WIDE], BF16, tag="a_grp", name="a_grp%d" % c, align_bytes=64)
+            g_grp = grp.tile([P, WIDE], BF16, tag="g_grp", name="g_grp%d" % c, align_bytes=64)
+            grouped[c] = (a_grp, g_grp)
+            if c == 0:
+                for dst, src in ((a_grp, a_raw[c]), (g_grp, g_raw[c])):
+                    nc.vector.tensor_tensor(
+                        out=dst[:].rearrange("p (w t) -> p w t", t=PACK),
+                        in0=src[:].rearrange("p (t w) -> p w t", t=PACK),
+                        in1=in_mask_wt,
+                        op=ALU.mult,
+                    )
+            else:
+                dst, src = regroup_views(a_grp[:], a_raw[c][:])
+                nc.scalar.copy(out=dst, in_=src)
+                dst, src = regroup_views(g_grp[:], g_raw[c][:])
+                nc.vector.tensor_copy(out=dst, in_=src)
+
+        def quantise_and_multiply(c, first, last):
+            a_grp, g_grp = grouped[c]
+            a_codes = mx.tile([P, COLS], U32, tag="a_codes", name="a_codes%d" % c, align_bytes=64)
+            a_scales = mx.tile([P, COLS], U8, tag="a_scales", name="a_scales%d" % c, align_bytes=64)
+            g_codes = mx.tile([P, COLS], U32, tag="g_codes", name="g_codes%d" % c, align_bytes=64)
+            g_scales = mx.tile([P, COLS], U8, tag="g_scales", name="g_scales%d" % c, align_bytes=64)
+            nc.vector.quantize_mx(out=a_codes[:].bitcast(E4M3X4), scales=a_scales[:], in_=a_grp[:])
+            nc.vector.quantize_mx(out=g_codes[:].bitcast(E5M2X4), scales=g_scales[:], in_=g_grp[:])
+            for m in reversed(range(M_TILES)):
+                cols = slice(m * P, (m + 1) * P)
+                nc.tensor.matmul_mx(
+                    out=acc[m][:],
+                    lhsT=a_codes[:, cols].bitcast(E4M3X4),
+                    lhsT_scale=a_scales[:, cols],
+                    rhs=g_codes[:].bitcast(E5M2X4),
+                    rhs_scale=g_scales[:],
+                    start=first,
+                    stop=last,
+                )
+
+        for idx, c in enumerate(PASS_ORDER):
+            regroup(c)
+            if idx > 0:
+                quantise_and_multiply(PASS_ORDER[idx - 1], idx == 1, False)
+        quantise_and_multiply(PASS_ORDER[-1], False, True)
+
+        for m in reversed(range(M_TILES)):
+            kept = (m + 1) * P
+            nc.vector.tensor_tensor(
+                out=out_sb[:, m, 0:kept],
+                in0=acc[m][:, 0:kept],
+                in1=out_mask[:, COLS - kept : COLS],
+                op=ALU.mult,
+            )
+            nc.sync.dma_start(out=out_rows[m], in_=out_sb[:, m, :])

@@ -15,102 +15,131 @@ PACK = 4
 K_PASS = P * PACK
 ROWS = 8192
 COLS = 512
+HALF = COLS // 2
 PASSES = ROWS // K_PASS
 M_TILES = COLS // P
 WIDE = PACK * COLS
+DIAG_PITCH = COLS + P
 
 FLOPS = 2 * ROWS * COLS * COLS
 BYTES = 2 * ROWS * COLS * 2 + COLS * COLS * 4
 
-PASS_ORDER = [1, 2, 0] + list(range(3, PASSES))
+PASS_ORDER = [1, 2, 3, 0] + list(range(4, PASSES))
+G_ON_SCALAR = (10,)
 
 
-def regroup_views(dst, src):
-    return (
-        dst.rearrange("p (c i t) -> p c t i", i=4, t=PACK),
-        src.rearrange("p (t c i) -> p c t i", t=PACK, i=4),
+def regroup(engine_copy, dst, src, col0, ncols):
+    engine_copy(
+        out=dst[:, PACK * col0 : PACK * (col0 + ncols)].rearrange("p (c i t) -> p c t i", i=4, t=PACK),
+        in_=src[:, 0:WIDE]
+        .rearrange("p (t w) -> p t w", t=PACK)[:, :, col0 : col0 + ncols]
+        .rearrange("p t (c i) -> p c t i", i=4),
     )
 
 
 def tile_modelnew_t_kernel(tc, A, B, grad_out, out):
     nc = tc.nc
-    a_rows = A.rearrange("(c p j) w -> c p (j w)", p=P, j=PACK)
-    g_rows = grad_out.rearrange("(c p j) w -> c p (j w)", p=P, j=PACK)
-    out_rows = out.rearrange("(m p) n -> m p n", p=P)
+    a_rows = A.rearrange("(c p j) w -> c p j w", p=P, j=PACK)
+    g_rows = grad_out.rearrange("(c p j) w -> c p j w", p=P, j=PACK)
 
     with ExitStack() as ctx:
         const = ctx.enter_context(tc.tile_pool(name="const", bufs=1))
-        raw = ctx.enter_context(tc.tile_pool(name="raw", bufs=PASSES))
-        grp = ctx.enter_context(tc.tile_pool(name="grp", bufs=3))
+        raw = ctx.enter_context(tc.tile_pool(name="raw", bufs=PASSES - 1))
+        grp = ctx.enter_context(tc.tile_pool(name="grp", bufs=4))
         mx = ctx.enter_context(tc.tile_pool(name="mx", bufs=3))
         psum = ctx.enter_context(tc.psum_pool(name="psum", bufs=1))
         ctx.enter_context(tc.manual_schedule())
 
         a_raw = {}
         g_raw = {}
-        for c in PASS_ORDER:
-            a_raw[c] = raw.tile([P, WIDE], BF16, tag="a_raw", name="a_raw%d" % c)
-            nc.sync.dma_start(out=a_raw[c][:], in_=a_rows[c])
-            g_raw[c] = raw.tile([P, WIDE], BF16, tag="g_raw", name="g_raw%d" % c)
-            nc.sync.dma_start(out=g_raw[c][:], in_=g_rows[c])
-
-        in_mask = const.tile([P, WIDE], F32, name="in_mask")
-        out_mask = const.tile([P, COLS], F32, name="out_mask")
-        out_sb = const.tile([P, M_TILES, COLS], F32, name="out_sb")
-        nc.vector.memset(in_mask[:], 1.0)
+        a_raw[0] = const.tile([P, PACK * DIAG_PITCH], BF16, name="a_raw_first")
+        g_raw[0] = const.tile([P, PACK * DIAG_PITCH], BF16, name="g_raw_first")
+        out_mask = const.tile([P, 2 * P], F32, name="out_mask")
+        tri_bf = const.tile([P, P], BF16, name="tri_bf")
+        zeros = const.tile([P, COLS - P], F32, name="zeros")
         nc.vector.memset(out_mask[:], 1.0)
-        nc.vector.memset(out_sb[:], 0.0)
-        in_mask_wt = in_mask[:].rearrange("p (w t) -> p w t", t=PACK)
-        nc.gpsimd.affine_select(
-            out=in_mask_wt,
-            in_=in_mask_wt,
-            pattern=[[-1, COLS], [1, PACK]],
-            compare_op=ALU.is_ge,
-            fill=0.0,
-            base=0,
-            channel_multiplier=PACK,
-        )
+        nc.vector.memset(a_raw[0][:], 0.0)
+        nc.vector.memset(g_raw[0][:], 0.0)
+        nc.vector.memset(zeros[:], 0.0)
         nc.gpsimd.affine_select(
             out=out_mask[:],
             in_=out_mask[:],
-            pattern=[[-1, COLS]],
+            pattern=[[-1, 2 * P]],
             compare_op=ALU.is_ge,
             fill=0.0,
-            base=COLS - P,
+            base=P,
             channel_multiplier=1,
         )
+        tri_f32 = out_mask[:, P : 2 * P]
+        nc.vector.tensor_copy(out=tri_bf[:], in_=tri_f32)
+
+        def load_cols(dst, rows, c, col0, ncols):
+            nc.sync.dma_start(
+                out=dst[:].rearrange("p (j w) -> p j w", j=PACK)[:, :, col0 : col0 + ncols],
+                in_=rows[c][:, :, col0 : col0 + ncols],
+            )
+
+        def load_first_pass_planes(dst, x, planes):
+            for t in planes:
+                kept = (t + 1) * P
+                nc.sync.dma_start(out=dst[:, t * COLS : t * COLS + kept], in_=x[t * P : (t + 1) * P, 0:kept])
+
+        for idx, c in enumerate(PASS_ORDER):
+            if c == 0:
+                continue
+            a_raw[c] = raw.tile([P, WIDE], BF16, tag="a_raw", name="a_raw%d" % c)
+            g_raw[c] = raw.tile([P, WIDE], BF16, tag="g_raw", name="g_raw%d" % c)
+            if idx == 0:
+                for h in range(2):
+                    load_cols(g_raw[c], g_rows, c, h * HALF, HALF)
+                    load_cols(a_raw[c], a_rows, c, h * HALF, HALF)
+            elif idx == PASSES - 1:
+                load_cols(g_raw[c], g_rows, c, 0, COLS)
+                load_cols(a_raw[c], a_rows, c, HALF, HALF)
+                load_cols(a_raw[c], a_rows, c, 0, HALF)
+            else:
+                load_cols(g_raw[c], g_rows, c, 0, COLS)
+                if idx in (1, 2):
+                    load_first_pass_planes(a_raw[0], A, (2 * idx - 2, 2 * idx - 1))
+                load_cols(a_raw[c], a_rows, c, 0, COLS)
+                if idx in (1, 2):
+                    load_first_pass_planes(g_raw[0], grad_out, (2 * idx - 2, 2 * idx - 1))
+        for m in range(M_TILES - 1):
+            kept = (m + 1) * P
+            nc.sync.dma_start(out=out[m * P : (m + 1) * P, kept:COLS], in_=zeros[:, 0 : COLS - kept])
 
         acc = [psum.tile([P, COLS], F32, name="acc%d" % m) for m in range(M_TILES)]
-
         grouped = {}
+        quantised = {}
 
-        def regroup(c):
-            a_grp = grp.tile([P, WIDE], BF16, tag="a_grp", name="a_grp%d" % c, align_bytes=64)
-            g_grp = grp.tile([P, WIDE], BF16, tag="g_grp", name="g_grp%d" % c, align_bytes=64)
-            grouped[c] = (a_grp, g_grp)
-            if c == 0:
-                for dst, src in ((a_grp, a_raw[c]), (g_grp, g_raw[c])):
-                    nc.vector.tensor_tensor(
-                        out=dst[:].rearrange("p (w t) -> p w t", t=PACK),
-                        in0=src[:].rearrange("p (t w) -> p w t", t=PACK),
-                        in1=in_mask_wt,
-                        op=ALU.mult,
-                    )
-            else:
-                dst, src = regroup_views(a_grp[:], a_raw[c][:])
-                nc.scalar.copy(out=dst, in_=src)
-                dst, src = regroup_views(g_grp[:], g_raw[c][:])
-                nc.vector.tensor_copy(out=dst, in_=src)
+        def new_tiles(c):
+            grouped[c] = (
+                grp.tile([P, WIDE], BF16, tag="a_grp", name="a_grp%d" % c, align_bytes=64),
+                grp.tile([P, WIDE], BF16, tag="g_grp", name="g_grp%d" % c, align_bytes=64),
+            )
+            quantised[c] = (
+                mx.tile([P, COLS], U32, tag="a_codes", name="a_codes%d" % c, align_bytes=64),
+                mx.tile([P, COLS], U8, tag="a_scales", name="a_scales%d" % c, align_bytes=64),
+                mx.tile([P, COLS], U32, tag="g_codes", name="g_codes%d" % c, align_bytes=64),
+                mx.tile([P, COLS], U8, tag="g_scales", name="g_scales%d" % c, align_bytes=64),
+            )
 
-        def quantise_and_multiply(c, first, last):
-            a_grp, g_grp = grouped[c]
-            a_codes = mx.tile([P, COLS], U32, tag="a_codes", name="a_codes%d" % c, align_bytes=64)
-            a_scales = mx.tile([P, COLS], U8, tag="a_scales", name="a_scales%d" % c, align_bytes=64)
-            g_codes = mx.tile([P, COLS], U32, tag="g_codes", name="g_codes%d" % c, align_bytes=64)
-            g_scales = mx.tile([P, COLS], U8, tag="g_scales", name="g_scales%d" % c, align_bytes=64)
-            nc.vector.quantize_mx(out=a_codes[:].bitcast(E4M3X4), scales=a_scales[:], in_=a_grp[:])
-            nc.vector.quantize_mx(out=g_codes[:].bitcast(E5M2X4), scales=g_scales[:], in_=g_grp[:])
-            for m in reversed(range(M_TILES)):
+        def quantise_a(c, col0, ncols):
+            cols = slice(col0, col0 + ncols)
+            nc.vector.quantize_mx(
+                out=quantised[c][0][:, cols].bitcast(E4M3X4),
+                scales=quantised[c][1][:, cols],
+                in_=grouped[c][0][:, PACK * col0 : PACK * (col0 + ncols)],
+            )
+
+        def quantise_g(c):
+            nc.vector.quantize_mx(
+                out=quantised[c][2][:].bitcast(E5M2X4), scales=quantised[c][3][:], in_=grouped[c][1][:]
+            )
+
+        def multiply(c, m_tiles, first, last):
+            a_codes, a_scales, g_codes, g_scales = quantised[c]
+            for m in m_tiles:
                 cols = slice(m * P, (m + 1) * P)
                 nc.tensor.matmul_mx(
                     out=acc[m][:],
@@ -123,17 +152,50 @@ def tile_modelnew_t_kernel(tc, A, B, grad_out, out):
                 )
 
         for idx, c in enumerate(PASS_ORDER):
-            regroup(c)
+            new_tiles(c)
+            a_grp, g_grp = grouped[c]
+            if idx == 0:
+                for h in range(2):
+                    regroup(nc.vector.tensor_copy, g_grp, g_raw[c], h * HALF, HALF)
+                    regroup(nc.scalar.copy, a_grp, a_raw[c], h * HALF, HALF)
+            elif idx == PASSES - 1:
+                regroup(nc.vector.tensor_copy, g_grp, g_raw[c], 0, COLS)
+                regroup(nc.scalar.copy, a_grp, a_raw[c], HALF, HALF)
+            else:
+                regroup(nc.scalar.copy, a_grp, a_raw[c], 0, COLS)
+                regroup(nc.scalar.copy if c in G_ON_SCALAR else nc.vector.tensor_copy, g_grp, g_raw[c], 0, COLS)
+            if idx + 1 < PASSES and PASS_ORDER[idx + 1] == 0:
+                for x in (a_raw[0], g_raw[0]):
+                    diag = x[:].rearrange("p (t r) -> p t r", r=DIAG_PITCH)[:, :, 0:P]
+                    nc.vector.tensor_tensor(
+                        out=diag, in0=diag, in1=tri_bf[:].unsqueeze(1).to_broadcast([P, PACK, P]), op=ALU.mult
+                    )
             if idx > 0:
-                quantise_and_multiply(PASS_ORDER[idx - 1], idx == 1, False)
-        quantise_and_multiply(PASS_ORDER[-1], False, True)
+                prev = PASS_ORDER[idx - 1]
+                quantise_a(prev, 0, COLS)
+                quantise_g(prev)
+                multiply(prev, (3, 2, 1, 0), idx == 1, False)
 
-        for m in reversed(range(M_TILES)):
-            kept = (m + 1) * P
-            nc.vector.tensor_tensor(
-                out=out_sb[:, m, 0:kept],
-                in0=acc[m][:, 0:kept],
-                in1=out_mask[:, COLS - kept : COLS],
-                op=ALU.mult,
-            )
-            nc.sync.dma_start(out=out_rows[m], in_=out_sb[:, m, :])
+        c = PASS_ORDER[-1]
+        regroup(nc.vector.tensor_copy, grouped[c][0], a_raw[c], 0, HALF)
+        quantise_g(c)
+        quantise_a(c, HALF, HALF)
+        multiply(c, (3, 2), False, True)
+        quantise_a(c, 0, HALF)
+        multiply(c, (1, 0), False, True)
+
+        out_sb = [const.tile([P, (m + 1) * P], F32, name="out_sb%d" % m) for m in range(M_TILES)]
+        nc.scalar.copy(out=out_sb[3][:], in_=acc[3][:])
+        nc.scalar.copy(out=out_sb[2][:], in_=acc[2][:, 0 : 3 * P])
+
+        def store(m):
+            nc.sync.dma_start(out=out[m * P : (m + 1) * P, 0 : (m + 1) * P], in_=out_sb[m][:])
+
+        nc.vector.tensor_tensor(out=out_sb[3][:, 3 * P : 4 * P], in0=out_sb[3][:, 3 * P : 4 * P], in1=tri_f32, op=ALU.mult)
+        store(3)
+        nc.vector.tensor_tensor(out=out_sb[1][:], in0=acc[1][:, 0 : 2 * P], in1=out_mask[:], op=ALU.mult)
+        store(1)
+        nc.vector.tensor_tensor(out=out_sb[2][:, 2 * P : 3 * P], in0=out_sb[2][:, 2 * P : 3 * P], in1=tri_f32, op=ALU.mult)
+        store(2)
+        nc.vector.tensor_tensor(out=out_sb[0][:], in0=acc[0][:, 0:P], in1=tri_f32, op=ALU.mult)
+        store(0)

@@ -1,6 +1,7 @@
 from contextlib import ExitStack
 
 import concourse.mybir as mybir
+from concourse.masks import make_identity
 
 BF16 = mybir.dt.bfloat16
 F32 = mybir.dt.float32
@@ -24,8 +25,9 @@ DIAG_PITCH = COLS + P
 FLOPS = 2 * ROWS * COLS * COLS
 BYTES = 2 * ROWS * COLS * 2 + COLS * COLS * 4
 
-PASS_ORDER = [1, 2, 3, 0] + list(range(4, PASSES))
-G_ON_SCALAR = (10,)
+VIA_PE = tuple(range(2, 14))
+G_COLS_ON_SCALAR = 96
+LAST_A_COLS_ON_SCALAR = 192
 
 
 def regroup(engine_copy, dst, src, col0, ncols):
@@ -39,8 +41,8 @@ def regroup(engine_copy, dst, src, col0, ncols):
 
 def tile_modelnew_t_kernel(tc, A, B, grad_out, out):
     nc = tc.nc
-    a_rows = A.rearrange("(c p j) w -> c p j w", p=P, j=PACK)
-    g_rows = grad_out.rearrange("(c p j) w -> c p j w", p=P, j=PACK)
+    a_rows = A.rearrange("(c p j) w -> c p (j w)", p=P, j=PACK)
+    g_rows = grad_out.rearrange("(c p j) w -> c p (j w)", p=P, j=PACK)
 
     with ExitStack() as ctx:
         const = ctx.enter_context(tc.tile_pool(name="const", bufs=1))
@@ -57,10 +59,23 @@ def tile_modelnew_t_kernel(tc, A, B, grad_out, out):
         out_mask = const.tile([P, 2 * P], F32, name="out_mask")
         tri_bf = const.tile([P, P], BF16, name="tri_bf")
         zeros = const.tile([P, COLS - P], F32, name="zeros")
-        nc.vector.memset(out_mask[:], 1.0)
-        nc.vector.memset(a_raw[0][:], 0.0)
-        nc.vector.memset(g_raw[0][:], 0.0)
-        nc.vector.memset(zeros[:], 0.0)
+        ident = const.tile([P, P], BF16, name="ident")
+
+        for x_raw, x in ((a_raw[0], A), (g_raw[0], grad_out)):
+            for t in range(PACK):
+                kept = (t + 1) * P
+                nc.sync.dma_start(out=x_raw[:, t * COLS : t * COLS + kept], in_=x[t * P : (t + 1) * P, 0:kept])
+        for c in range(1, PASSES):
+            a_raw[c] = raw.tile([P, WIDE], BF16, tag="a_raw", name="a_raw%d" % c)
+            g_raw[c] = raw.tile([P, WIDE], BF16, tag="g_raw", name="g_raw%d" % c)
+            if c < PASSES - 1:
+                nc.sync.dma_start(out=a_raw[c][:], in_=a_rows[c])
+                nc.sync.dma_start(out=g_raw[c][:], in_=g_rows[c])
+            else:
+                nc.sync.dma_start(out=g_raw[c][:], in_=g_rows[c])
+                nc.sync.dma_start(out=a_raw[c][:], in_=a_rows[c])
+
+        nc.gpsimd.memset(out_mask[:], 1.0)
         nc.gpsimd.affine_select(
             out=out_mask[:],
             in_=out_mask[:],
@@ -70,40 +85,13 @@ def tile_modelnew_t_kernel(tc, A, B, grad_out, out):
             base=P,
             channel_multiplier=1,
         )
+        make_identity(nc, ident[:])
         tri_f32 = out_mask[:, P : 2 * P]
+        for x_raw in (a_raw[0], g_raw[0]):
+            for t in range(PACK - 1):
+                nc.vector.memset(x_raw[:, t * COLS + (t + 1) * P : (t + 1) * COLS], 0.0)
+        nc.vector.memset(zeros[:], 0.0)
         nc.vector.tensor_copy(out=tri_bf[:], in_=tri_f32)
-
-        def load_cols(dst, rows, c, col0, ncols):
-            nc.sync.dma_start(
-                out=dst[:].rearrange("p (j w) -> p j w", j=PACK)[:, :, col0 : col0 + ncols],
-                in_=rows[c][:, :, col0 : col0 + ncols],
-            )
-
-        def load_first_pass_planes(dst, x, planes):
-            for t in planes:
-                kept = (t + 1) * P
-                nc.sync.dma_start(out=dst[:, t * COLS : t * COLS + kept], in_=x[t * P : (t + 1) * P, 0:kept])
-
-        for idx, c in enumerate(PASS_ORDER):
-            if c == 0:
-                continue
-            a_raw[c] = raw.tile([P, WIDE], BF16, tag="a_raw", name="a_raw%d" % c)
-            g_raw[c] = raw.tile([P, WIDE], BF16, tag="g_raw", name="g_raw%d" % c)
-            if idx == 0:
-                for h in range(2):
-                    load_cols(g_raw[c], g_rows, c, h * HALF, HALF)
-                    load_cols(a_raw[c], a_rows, c, h * HALF, HALF)
-            elif idx == PASSES - 1:
-                load_cols(g_raw[c], g_rows, c, 0, COLS)
-                load_cols(a_raw[c], a_rows, c, HALF, HALF)
-                load_cols(a_raw[c], a_rows, c, 0, HALF)
-            else:
-                load_cols(g_raw[c], g_rows, c, 0, COLS)
-                if idx in (1, 2):
-                    load_first_pass_planes(a_raw[0], A, (2 * idx - 2, 2 * idx - 1))
-                load_cols(a_raw[c], a_rows, c, 0, COLS)
-                if idx in (1, 2):
-                    load_first_pass_planes(g_raw[0], grad_out, (2 * idx - 2, 2 * idx - 1))
         for m in range(M_TILES - 1):
             kept = (m + 1) * P
             nc.sync.dma_start(out=out[m * P : (m + 1) * P, kept:COLS], in_=zeros[:, 0 : COLS - kept])
@@ -111,6 +99,7 @@ def tile_modelnew_t_kernel(tc, A, B, grad_out, out):
         acc = [psum.tile([P, COLS], F32, name="acc%d" % m) for m in range(M_TILES)]
         grouped = {}
         quantised = {}
+        passed = {}
 
         def new_tiles(c):
             grouped[c] = (
@@ -123,6 +112,19 @@ def tile_modelnew_t_kernel(tc, A, B, grad_out, out):
                 mx.tile([P, COLS], U32, tag="g_codes", name="g_codes%d" % c, align_bytes=64),
                 mx.tile([P, COLS], U8, tag="g_scales", name="g_scales%d" % c, align_bytes=64),
             )
+
+        def pass_through(c):
+            passed[c] = psum.tile([P, PACK * HALF], BF16, tag="passed", name="passed%d" % c, bufs=4)
+            by_t = passed[c][:].rearrange("p (w t) -> p t w", t=PACK)
+            planes = a_raw[c][:].rearrange("p (t w) -> p t w", t=PACK)
+            for t in range(0, PACK, 2):
+                nc.tensor.matmul(
+                    out=by_t[:, t : t + 2, :],
+                    lhsT=ident[:],
+                    rhs=planes[:, t : t + 2, 0:HALF],
+                    start=True,
+                    stop=True,
+                )
 
         def quantise_a(c, col0, ncols):
             cols = slice(col0, col0 + ncols)
@@ -151,38 +153,40 @@ def tile_modelnew_t_kernel(tc, A, B, grad_out, out):
                     stop=last,
                 )
 
-        for idx, c in enumerate(PASS_ORDER):
+        for c in range(PASSES):
             new_tiles(c)
             a_grp, g_grp = grouped[c]
-            if idx == 0:
-                for h in range(2):
-                    regroup(nc.vector.tensor_copy, g_grp, g_raw[c], h * HALF, HALF)
-                    regroup(nc.scalar.copy, a_grp, a_raw[c], h * HALF, HALF)
-            elif idx == PASSES - 1:
-                regroup(nc.vector.tensor_copy, g_grp, g_raw[c], 0, COLS)
-                regroup(nc.scalar.copy, a_grp, a_raw[c], HALF, HALF)
-            else:
-                regroup(nc.scalar.copy, a_grp, a_raw[c], 0, COLS)
-                regroup(nc.scalar.copy if c in G_ON_SCALAR else nc.vector.tensor_copy, g_grp, g_raw[c], 0, COLS)
-            if idx + 1 < PASSES and PASS_ORDER[idx + 1] == 0:
-                for x in (a_raw[0], g_raw[0]):
-                    diag = x[:].rearrange("p (t r) -> p t r", r=DIAG_PITCH)[:, :, 0:P]
+            if c + 1 in VIA_PE:
+                pass_through(c + 1)
+            if c == 0:
+                for x_raw in (a_raw[0], g_raw[0]):
+                    diag = x_raw[:].rearrange("p (t r) -> p t r", r=DIAG_PITCH)[:, :, 0:P]
                     nc.vector.tensor_tensor(
                         out=diag, in0=diag, in1=tri_bf[:].unsqueeze(1).to_broadcast([P, PACK, P]), op=ALU.mult
                     )
-            if idx > 0:
-                prev = PASS_ORDER[idx - 1]
-                quantise_a(prev, 0, COLS)
-                quantise_g(prev)
-                multiply(prev, (3, 2, 1, 0), idx == 1, False)
-
-        c = PASS_ORDER[-1]
-        regroup(nc.vector.tensor_copy, grouped[c][0], a_raw[c], 0, HALF)
-        quantise_g(c)
-        quantise_a(c, HALF, HALF)
-        multiply(c, (3, 2), False, True)
-        quantise_a(c, 0, HALF)
-        multiply(c, (1, 0), False, True)
+            if c == PASSES - 1:
+                split = LAST_A_COLS_ON_SCALAR
+                regroup(nc.vector.tensor_copy, g_grp, g_raw[c], 0, COLS)
+                regroup(nc.scalar.copy, a_grp, a_raw[c], 0, split)
+                regroup(nc.vector.tensor_copy, a_grp, a_raw[c], split, COLS - split)
+                quantise_g(c)
+                quantise_a(c, HALF, HALF)
+                multiply(c, (3, 2), False, True)
+                quantise_a(c, 0, HALF)
+                multiply(c, (1, 0), False, True)
+            else:
+                if c in VIA_PE:
+                    split = COLS - G_COLS_ON_SCALAR
+                    regroup(nc.scalar.copy, a_grp, a_raw[c], HALF, HALF)
+                    nc.scalar.copy(out=a_grp[:, 0 : PACK * HALF], in_=passed[c][:])
+                    regroup(nc.vector.tensor_copy, g_grp, g_raw[c], 0, split)
+                    regroup(nc.scalar.copy, g_grp, g_raw[c], split, COLS - split)
+                else:
+                    regroup(nc.scalar.copy, a_grp, a_raw[c], 0, COLS)
+                    regroup(nc.vector.tensor_copy, g_grp, g_raw[c], 0, COLS)
+                quantise_a(c, 0, COLS)
+                quantise_g(c)
+                multiply(c, (3, 2, 1, 0), c == 0, False)
 
         out_sb = [const.tile([P, (m + 1) * P], F32, name="out_sb%d" % m) for m in range(M_TILES)]
         nc.scalar.copy(out=out_sb[3][:], in_=acc[3][:])

@@ -26,7 +26,7 @@ FLOPS = 2 * ROWS * COLS * COLS
 BYTES = 2 * ROWS * COLS * 2 + COLS * COLS * 4
 
 VIA_PE = tuple(range(2, 14))
-G_COLS_ON_SCALAR = 96
+G_COLS_ON_SCALAR = 0
 LAST_A_COLS_ON_SCALAR = 192
 
 
@@ -180,7 +180,8 @@ def tile_modelnew_t_kernel(tc, A, B, grad_out, out):
                     regroup(nc.scalar.copy, a_grp, a_raw[c], HALF, HALF)
                     nc.scalar.copy(out=a_grp[:, 0 : PACK * HALF], in_=passed[c][:])
                     regroup(nc.vector.tensor_copy, g_grp, g_raw[c], 0, split)
-                    regroup(nc.scalar.copy, g_grp, g_raw[c], split, COLS - split)
+                    if split < COLS:
+                        regroup(nc.scalar.copy, g_grp, g_raw[c], split, COLS - split)
                 else:
                     regroup(nc.scalar.copy, a_grp, a_raw[c], 0, COLS)
                     regroup(nc.vector.tensor_copy, g_grp, g_raw[c], 0, COLS)

@@ -26,8 +26,7 @@ FLOPS = 2 * ROWS * COLS * COLS
 BYTES = 2 * ROWS * COLS * 2 + COLS * COLS * 4
 
 VIA_PE = tuple(range(2, 14))
-G_COLS_ON_SCALAR = 0
-LAST_A_COLS_ON_SCALAR = 192
+G_COLS_ON_SCALAR = 48
 
 
 def regroup(engine_copy, dst, src, col0, ncols):
@@ -47,8 +46,8 @@ def tile_modelnew_t_kernel(tc, A, B, grad_out, out):
     with ExitStack() as ctx:
         const = ctx.enter_context(tc.tile_pool(name="const", bufs=1))
         raw = ctx.enter_context(tc.tile_pool(name="raw", bufs=PASSES - 1))
-        grp = ctx.enter_context(tc.tile_pool(name="grp", bufs=4))
-        mx = ctx.enter_context(tc.tile_pool(name="mx", bufs=3))
+        grp = ctx.enter_context(tc.tile_pool(name="grp", bufs=6))
+        mx = ctx.enter_context(tc.tile_pool(name="mx", bufs=4))
         psum = ctx.enter_context(tc.psum_pool(name="psum", bufs=1))
         ctx.enter_context(tc.manual_schedule())
 
@@ -165,10 +164,9 @@ def tile_modelnew_t_kernel(tc, A, B, grad_out, out):
                         out=diag, in0=diag, in1=tri_bf[:].unsqueeze(1).to_broadcast([P, PACK, P]), op=ALU.mult
                     )
             if c == PASSES - 1:
-                split = LAST_A_COLS_ON_SCALAR
-                regroup(nc.vector.tensor_copy, g_grp, g_raw[c], 0, COLS)
-                regroup(nc.scalar.copy, a_grp, a_raw[c], 0, split)
-                regroup(nc.vector.tensor_copy, a_grp, a_raw[c], split, COLS - split)
+                regroup(nc.scalar.copy, g_grp, g_raw[c], 0, COLS)
+                regroup(nc.scalar.copy, a_grp, a_raw[c], 0, HALF)
+                regroup(nc.vector.tensor_copy, a_grp, a_raw[c], HALF, HALF)
                 quantise_g(c)
                 quantise_a(c, HALF, HALF)
                 multiply(c, (3, 2), False, True)

@@ -26,7 +26,7 @@ FLOPS = 2 * ROWS * COLS * COLS
 BYTES = 2 * ROWS * COLS * 2 + COLS * COLS * 4
 
 VIA_PE = tuple(range(2, 14))
-G_COLS_ON_SCALAR = 48
+G_COLS_ON_SCALAR = 80
 
 
 def regroup(engine_copy, dst, src, col0, ncols):
@@ -59,6 +59,10 @@ def tile_modelnew_t_kernel(tc, A, B, grad_out, out):
         tri_bf = const.tile([P, P], BF16, name="tri_bf")
         zeros = const.tile([P, COLS - P], F32, name="zeros")
         ident = const.tile([P, P], BF16, name="ident")
+        first_act = const.tile([P, 2], F32, name="first_act")
+
+        nc.vector.memset(first_act[:, 0:1], 0.0)
+        nc.scalar.copy(out=first_act[:, 1:2], in_=first_act[:, 0:1])
 
         for x_raw, x in ((a_raw[0], A), (g_raw[0], grad_out)):
             for t in range(PACK):
@@ -84,13 +88,14 @@ def tile_modelnew_t_kernel(tc, A, B, grad_out, out):
             base=P,
             channel_multiplier=1,
         )
-        make_identity(nc, ident[:])
         tri_f32 = out_mask[:, P : 2 * P]
-        for x_raw in (a_raw[0], g_raw[0]):
-            for t in range(PACK - 1):
-                nc.vector.memset(x_raw[:, t * COLS + (t + 1) * P : (t + 1) * COLS], 0.0)
-        nc.vector.memset(zeros[:], 0.0)
+        for t in range(PACK - 1):
+            nc.vector.memset(a_raw[0][:, t * COLS + (t + 1) * P : (t + 1) * COLS], 0.0)
         nc.vector.tensor_copy(out=tri_bf[:], in_=tri_f32)
+        for t in range(PACK - 1):
+            nc.gpsimd.memset(g_raw[0][:, t * COLS + (t + 1) * P : (t + 1) * COLS], 0.0)
+        make_identity(nc, ident[:])
+        nc.gpsimd.memset(zeros[:], 0.0)
         for m in range(M_TILES - 1):
             kept = (m + 1) * P
             nc.sync.dma_start(out=out[m * P : (m + 1) * P, kept:COLS], in_=zeros[:, 0 : COLS - kept])
@@ -138,16 +143,16 @@ def tile_modelnew_t_kernel(tc, A, B, grad_out, out):
                 out=quantised[c][2][:].bitcast(E5M2X4), scales=quantised[c][3][:], in_=grouped[c][1][:]
             )
 
-        def multiply(c, m_tiles, first, last):
+        def multiply(c, widths, first, last):
             a_codes, a_scales, g_codes, g_scales = quantised[c]
-            for m in m_tiles:
+            for m, n in widths:
                 cols = slice(m * P, (m + 1) * P)
                 nc.tensor.matmul_mx(
-                    out=acc[m][:],
+                    out=acc[m][:, 0:n],
                     lhsT=a_codes[:, cols].bitcast(E4M3X4),
                     lhsT_scale=a_scales[:, cols],
-                    rhs=g_codes[:].bitcast(E5M2X4),
-                    rhs_scale=g_scales[:],
+                    rhs=g_codes[:, 0:n].bitcast(E5M2X4),
+                    rhs_scale=g_scales[:, 0:n],
                     start=first,
                     stop=last,
                 )
@@ -166,39 +171,46 @@ def tile_modelnew_t_kernel(tc, A, B, grad_out, out):
             if c == PASSES - 1:
                 regroup(nc.scalar.copy, g_grp, g_raw[c], 0, COLS)
                 regroup(nc.scalar.copy, a_grp, a_raw[c], 0, HALF)
+                quantise_a(c - 1, 0, COLS)
+                quantise_g(c - 1)
+                multiply(c - 1, [(m, COLS) for m in (3, 2, 1, 0)], False, False)
                 regroup(nc.vector.tensor_copy, a_grp, a_raw[c], HALF, HALF)
                 quantise_g(c)
                 quantise_a(c, HALF, HALF)
-                multiply(c, (3, 2), False, True)
+                multiply(c, ((3, COLS), (2, COLS)), False, True)
                 quantise_a(c, 0, HALF)
-                multiply(c, (1, 0), False, True)
+                multiply(c, ((1, COLS), (0, COLS)), False, True)
             else:
                 if c in VIA_PE:
                     split = COLS - G_COLS_ON_SCALAR
                     regroup(nc.scalar.copy, a_grp, a_raw[c], HALF, HALF)
                     nc.scalar.copy(out=a_grp[:, 0 : PACK * HALF], in_=passed[c][:])
+                    regroup(nc.scalar.copy, g_grp, g_raw[c], split, COLS - split)
                     regroup(nc.vector.tensor_copy, g_grp, g_raw[c], 0, split)
-                    if split < COLS:
-                        regroup(nc.scalar.copy, g_grp, g_raw[c], split, COLS - split)
                 else:
                     regroup(nc.scalar.copy, a_grp, a_raw[c], 0, COLS)
                     regroup(nc.vector.tensor_copy, g_grp, g_raw[c], 0, COLS)
-                quantise_a(c, 0, COLS)
-                quantise_g(c)
-                multiply(c, (3, 2, 1, 0), c == 0, False)
+                if c > 0:
+                    quantise_a(c - 1, 0, COLS)
+                    quantise_g(c - 1)
+                    multiply(c - 1, [(m, COLS) for m in (3, 2, 1, 0)], c == 1, False)
 
         out_sb = [const.tile([P, (m + 1) * P], F32, name="out_sb%d" % m) for m in range(M_TILES)]
-        nc.scalar.copy(out=out_sb[3][:], in_=acc[3][:])
-        nc.scalar.copy(out=out_sb[2][:], in_=acc[2][:, 0 : 3 * P])
 
         def store(m):
             nc.sync.dma_start(out=out[m * P : (m + 1) * P, 0 : (m + 1) * P], in_=out_sb[m][:])
 
-        nc.vector.tensor_tensor(out=out_sb[3][:, 3 * P : 4 * P], in0=out_sb[3][:, 3 * P : 4 * P], in1=tri_f32, op=ALU.mult)
+        def mask_diagonal(m):
+            block = slice(m * P, (m + 1) * P)
+            nc.vector.tensor_tensor(out=out_sb[m][:, block], in0=acc[m][:, block], in1=tri_f32, op=ALU.mult)
+
+        mask_diagonal(3)
+        nc.scalar.copy(out=out_sb[3][:, 0 : 3 * P], in_=acc[3][:, 0 : 3 * P])
         store(3)
+        mask_diagonal(2)
+        nc.scalar.copy(out=out_sb[2][:, 0 : 2 * P], in_=acc[2][:, 0 : 2 * P])
+        store(2)
         nc.vector.tensor_tensor(out=out_sb[1][:], in0=acc[1][:, 0 : 2 * P], in1=out_mask[:], op=ALU.mult)
         store(1)
-        nc.vector.tensor_tensor(out=out_sb[2][:, 2 * P : 3 * P], in0=out_sb[2][:, 2 * P : 3 * P], in1=tri_f32, op=ALU.mult)
-        store(2)
-        nc.vector.tensor_tensor(out=out_sb[0][:], in0=acc[0][:, 0:P], in1=tri_f32, op=ALU.mult)
+        mask_diagonal(0)
         store(0)

@@ -26,7 +26,7 @@ FLOPS = 2 * ROWS * COLS * COLS
 BYTES = 2 * ROWS * COLS * 2 + COLS * COLS * 4
 
 VIA_PE = tuple(range(2, 14))
-G_COLS_ON_SCALAR = 80
+G_COLS_ON_SCALAR = 104
 
 
 def regroup(engine_copy, dst, src, col0, ncols):
@@ -101,6 +101,7 @@ def tile_modelnew_t_kernel(tc, A, B, grad_out, out):
             nc.sync.dma_start(out=out[m * P : (m + 1) * P, kept:COLS], in_=zeros[:, 0 : COLS - kept])
 
         acc = [psum.tile([P, COLS], F32, name="acc%d" % m) for m in range(M_TILES)]
+        out_sb = [const.tile([P, (m + 1) * P], F32, name="out_sb%d" % m) for m in range(M_TILES)]
         grouped = {}
         quantised = {}
         passed = {}
@@ -178,6 +179,8 @@ def tile_modelnew_t_kernel(tc, A, B, grad_out, out):
                 quantise_g(c)
                 quantise_a(c, HALF, HALF)
                 multiply(c, ((3, COLS), (2, COLS)), False, True)
+                for m in (3, 2):
+                    nc.scalar.copy(out=out_sb[m][:, 0 : m * P], in_=acc[m][:, 0 : m * P])
                 quantise_a(c, 0, HALF)
                 multiply(c, ((1, COLS), (0, COLS)), False, True)
             else:
@@ -195,8 +198,6 @@ def tile_modelnew_t_kernel(tc, A, B, grad_out, out):
                     quantise_g(c - 1)
                     multiply(c - 1, [(m, COLS) for m in (3, 2, 1, 0)], c == 1, False)
 
-        out_sb = [const.tile([P, (m + 1) * P], F32, name="out_sb%d" % m) for m in range(M_TILES)]
-
         def store(m):
             nc.sync.dma_start(out=out[m * P : (m + 1) * P, 0 : (m + 1) * P], in_=out_sb[m][:])
 
@@ -204,12 +205,9 @@ def tile_modelnew_t_kernel(tc, A, B, grad_out, out):
             block = slice(m * P, (m + 1) * P)
             nc.vector.tensor_tensor(out=out_sb[m][:, block], in0=acc[m][:, block], in1=tri_f32, op=ALU.mult)
 
-        mask_diagonal(3)
-        nc.scalar.copy(out=out_sb[3][:, 0 : 3 * P], in_=acc[3][:, 0 : 3 * P])
-        store(3)
-        mask_diagonal(2)
-        nc.scalar.copy(out=out_sb[2][:, 0 : 2 * P], in_=acc[2][:, 0 : 2 * P])
-        store(2)
+        for m in (3, 2):
+            mask_diagonal(m)
+            store(m)
         nc.vector.tensor_tensor(out=out_sb[1][:], in0=acc[1][:, 0 : 2 * P], in1=out_mask[:], op=ALU.mult)
         store(1)
         mask_diagonal(0)

@@ -25,7 +25,7 @@ DIAG_PITCH = COLS + P
 FLOPS = 2 * ROWS * COLS * COLS
 BYTES = 2 * ROWS * COLS * 2 + COLS * COLS * 4
 
-VIA_PE = tuple(range(2, 14))
+VIA_PE = tuple(range(3, 15))
 G_COLS_ON_SCALAR = 104
 
 
@@ -170,11 +170,9 @@ def tile_modelnew_t_kernel(tc, A, B, grad_out, out):
                         out=diag, in0=diag, in1=tri_bf[:].unsqueeze(1).to_broadcast([P, PACK, P]), op=ALU.mult
                     )
             if c == PASSES - 1:
-                regroup(nc.scalar.copy, g_grp, g_raw[c], 0, COLS)
+                regroup(nc.scalar.copy, g_grp, g_raw[c], P, COLS - P)
                 regroup(nc.scalar.copy, a_grp, a_raw[c], 0, HALF)
-                quantise_a(c - 1, 0, COLS)
-                quantise_g(c - 1)
-                multiply(c - 1, [(m, COLS) for m in (3, 2, 1, 0)], False, False)
+                regroup(nc.vector.tensor_copy, g_grp, g_raw[c], 0, P)
                 regroup(nc.vector.tensor_copy, a_grp, a_raw[c], HALF, HALF)
                 quantise_g(c)
                 quantise_a(c, HALF, HALF)
@@ -193,10 +191,10 @@ def tile_modelnew_t_kernel(tc, A, B, grad_out, out):
                 else:
                     regroup(nc.scalar.copy, a_grp, a_raw[c], 0, COLS)
                     regroup(nc.vector.tensor_copy, g_grp, g_raw[c], 0, COLS)
-                if c > 0:
-                    quantise_a(c - 1, 0, COLS)
-                    quantise_g(c - 1)
-                    multiply(c - 1, [(m, COLS) for m in (3, 2, 1, 0)], c == 1, False)
+                for b in {0: (), 1: (0, 1)}.get(c, (c,)):
+                    quantise_a(b, 0, COLS)
+                    quantise_g(b)
+                    multiply(b, [(m, COLS) for m in (3, 2, 1, 0)], b == 0, False)
 
         def store(m):
             nc.sync.dma_start(out=out[m * P : (m + 1) * P, 0 : (m + 1) * P], in_=out_sb[m][:])

@@ -26,6 +26,7 @@ FLOPS = 2 * ROWS * COLS * COLS
 BYTES = 2 * ROWS * COLS * 2 + COLS * COLS * 4
 
 VIA_PE = tuple(range(3, 15))
+CATCH_UP = 12
 G_COLS_ON_SCALAR = 104
 
 
@@ -161,8 +162,8 @@ def tile_modelnew_t_kernel(tc, A, B, grad_out, out):
         for c in range(PASSES):
             new_tiles(c)
             a_grp, g_grp = grouped[c]
-            if c + 1 in VIA_PE:
-                pass_through(c + 1)
+            if c + 2 in VIA_PE:
+                pass_through(c + 2)
             if c == 0:
                 for x_raw in (a_raw[0], g_raw[0]):
                     diag = x_raw[:].rearrange("p (t r) -> p t r", r=DIAG_PITCH)[:, :, 0:P]
@@ -191,7 +192,7 @@ def tile_modelnew_t_kernel(tc, A, B, grad_out, out):
                 else:
                     regroup(nc.scalar.copy, a_grp, a_raw[c], 0, COLS)
                     regroup(nc.vector.tensor_copy, g_grp, g_raw[c], 0, COLS)
-                for b in {0: (), 1: (0, 1)}.get(c, (c,)):
+                for b in range(c - (0 < c <= CATCH_UP), c + (c >= CATCH_UP)):
                     quantise_a(b, 0, COLS)
                     quantise_g(b)
                     multiply(b, [(m, COLS) for m in (3, 2, 1, 0)], b == 0, False)

@@ -25,8 +25,8 @@ DIAG_PITCH = COLS + P
 FLOPS = 2 * ROWS * COLS * COLS
 BYTES = 2 * ROWS * COLS * 2 + COLS * COLS * 4
 
-VIA_PE = tuple(range(3, 15))
-CATCH_UP = 12
+VIA_PE = tuple(range(2, 15, 2))
+CATCH_UP = 6
 G_COLS_ON_SCALAR = 104
 
 
@@ -176,9 +176,9 @@ def tile_modelnew_t_kernel(tc, A, B, grad_out, out):
                 regroup(nc.vector.tensor_copy, g_grp, g_raw[c], 0, P)
                 regroup(nc.vector.tensor_copy, a_grp, a_raw[c], HALF, HALF)
                 quantise_g(c)
-                quantise_a(c, HALF, HALF)
-                multiply(c, ((3, COLS), (2, COLS)), False, True)
                 for m in (3, 2):
+                    quantise_a(c, m * P, P)
+                    multiply(c, ((m, COLS),), False, True)
                     nc.scalar.copy(out=out_sb[m][:, 0 : m * P], in_=acc[m][:, 0 : m * P])
                 quantise_a(c, 0, HALF)
                 multiply(c, ((1, COLS), (0, COLS)), False, True)
@@ -205,8 +205,11 @@ def tile_modelnew_t_kernel(tc, A, B, grad_out, out):
             nc.vector.tensor_tensor(out=out_sb[m][:, block], in0=acc[m][:, block], in1=tri_f32, op=ALU.mult)
 
         for m in (3, 2):
+            nc.sync.dma_start(out=out[m * P : (m + 1) * P, 0 : m * P], in_=out_sb[m][:, 0 : m * P])
+        for m in (3, 2):
             mask_diagonal(m)
-            store(m)
+            block = slice(m * P, (m + 1) * P)
+            nc.sync.dma_start(out=out[block, block], in_=out_sb[m][:, block])
         nc.vector.tensor_tensor(out=out_sb[1][:], in0=acc[1][:, 0 : 2 * P], in1=out_mask[:], op=ALU.mult)
         store(1)
         mask_diagonal(0)

from contextlib import ExitStack

import concourse.mybir as mybir
from concourse.masks import make_identity

BF16 = mybir.dt.bfloat16
F32 = mybir.dt.float32
U32 = mybir.dt.uint32
U8 = mybir.dt.uint8
E4M3X4 = mybir.dt.float8_e4m3fn_x4
E5M2X4 = mybir.dt.float8_e5m2_x4
ALU = mybir.AluOpType

P = 128
PACK = 4
K_PASS = P * PACK
ROWS = 8192
COLS = 512
HALF = COLS // 2
PASSES = ROWS // K_PASS
M_TILES = COLS // P
WIDE = PACK * COLS
DIAG_PITCH = COLS + P

FLOPS = 2 * ROWS * COLS * COLS
BYTES = 2 * ROWS * COLS * 2 + COLS * COLS * 4

VIA_PE = tuple(range(2, 15, 2))
CATCH_UP = 6
G_COLS_ON_SCALAR = 104


def regroup(engine_copy, dst, src, col0, ncols):
    engine_copy(
        out=dst[:, PACK * col0 : PACK * (col0 + ncols)].rearrange("p (c i t) -> p c t i", i=4, t=PACK),
        in_=src[:, 0:WIDE]
        .rearrange("p (t w) -> p t w", t=PACK)[:, :, col0 : col0 + ncols]
        .rearrange("p t (c i) -> p c t i", i=4),
    )


def tile_modelnew_t_kernel(tc, A, B, grad_out, out):
    nc = tc.nc
    a_rows = A.rearrange("(c p j) w -> c p (j w)", p=P, j=PACK)
    g_rows = grad_out.rearrange("(c p j) w -> c p (j w)", p=P, j=PACK)

    with ExitStack() as ctx:
        const = ctx.enter_context(tc.tile_pool(name="const", bufs=1))
        raw = ctx.enter_context(tc.tile_pool(name="raw", bufs=PASSES - 1))
        grp = ctx.enter_context(tc.tile_pool(name="grp", bufs=6))
        mx = ctx.enter_context(tc.tile_pool(name="mx", bufs=4))
        psum = ctx.enter_context(tc.psum_pool(name="psum", bufs=1))
        ctx.enter_context(tc.manual_schedule())

        a_raw = {}
        g_raw = {}
        a_raw[0] = const.tile([P, PACK * DIAG_PITCH], BF16, name="a_raw_first")
        g_raw[0] = const.tile([P, PACK * DIAG_PITCH], BF16, name="g_raw_first")
        out_mask = const.tile([P, 2 * P], F32, name="out_mask")
        tri_bf = const.tile([P, P], BF16, name="tri_bf")
        zeros = const.tile([P, COLS - P], F32, name="zeros")
        ident = const.tile([P, P], BF16, name="ident")
        first_act = const.tile([P, 2], F32, name="first_act")

        nc.vector.memset(first_act[:, 0:1], 0.0)
        nc.scalar.copy(out=first_act[:, 1:2], in_=first_act[:, 0:1])

        for x_raw, x in ((a_raw[0], A), (g_raw[0], grad_out)):
            for t in range(PACK):
                kept = (t + 1) * P
                nc.sync.dma_start(out=x_raw[:, t * COLS : t * COLS + kept], in_=x[t * P : (t + 1) * P, 0:kept])
        for c in range(1, PASSES):
            a_raw[c] = raw.tile([P, WIDE], BF16, tag="a_raw", name="a_raw%d" % c)
            g_raw[c] = raw.tile([P, WIDE], BF16, tag="g_raw", name="g_raw%d" % c)
            if c < PASSES - 1:
                nc.sync.dma_start(out=a_raw[c][:], in_=a_rows[c])
                nc.sync.dma_start(out=g_raw[c][:], in_=g_rows[c])
            else:
                nc.sync.dma_start(out=g_raw[c][:], in_=g_rows[c])
                nc.sync.dma_start(out=a_raw[c][:], in_=a_rows[c])

        nc.gpsimd.memset(out_mask[:], 1.0)
        nc.gpsimd.affine_select(
            out=out_mask[:],
            in_=out_mask[:],
            pattern=[[-1, 2 * P]],
            compare_op=ALU.is_ge,
            fill=0.0,
            base=P,
            channel_multiplier=1,
        )
        tri_f32 = out_mask[:, P : 2 * P]
        for t in range(PACK - 1):
            nc.vector.memset(a_raw[0][:, t * COLS + (t + 1) * P : (t + 1) * COLS], 0.0)
        nc.vector.tensor_copy(out=tri_bf[:], in_=tri_f32)
        for t in range(PACK - 1):
            nc.gpsimd.memset(g_raw[0][:, t * COLS + (t + 1) * P : (t + 1) * COLS], 0.0)
        make_identity(nc, ident[:])
        nc.gpsimd.memset(zeros[:], 0.0)
        for m in range(M_TILES - 1):
            kept = (m + 1) * P
            nc.sync.dma_start(out=out[m * P : (m + 1) * P, kept:COLS], in_=zeros[:, 0 : COLS - kept])

        acc = [psum.tile([P, COLS], F32, name="acc%d" % m) for m in range(M_TILES)]
        out_sb = [const.tile([P, (m + 1) * P], F32, name="out_sb%d" % m) for m in range(M_TILES)]
        grouped = {}
        quantised = {}
        passed = {}

        def new_tiles(c):
            grouped[c] = (
                grp.tile([P, WIDE], BF16, tag="a_grp", name="a_grp%d" % c, align_bytes=64),
                grp.tile([P, WIDE], BF16, tag="g_grp", name="g_grp%d" % c, align_bytes=64),
            )
            quantised[c] = (
                mx.tile([P, COLS], U32, tag="a_codes", name="a_codes%d" % c, align_bytes=64),
                mx.tile([P, COLS], U8, tag="a_scales", name="a_scales%d" % c, align_bytes=64),
                mx.tile([P, COLS], U32, tag="g_codes", name="g_codes%d" % c, align_bytes=64),
                mx.tile([P, COLS], U8, tag="g_scales", name="g_scales%d" % c, align_bytes=64),
            )

        def pass_through(c):
            passed[c] = psum.tile([P, PACK * HALF], BF16, tag="passed", name="passed%d" % c, bufs=4)
            by_t = passed[c][:].rearrange("p (w t) -> p t w", t=PACK)
            planes = a_raw[c][:].rearrange("p (t w) -> p t w", t=PACK)
            for t in range(0, PACK, 2):
                nc.tensor.matmul(
                    out=by_t[:, t : t + 2, :],
                    lhsT=ident[:],
                    rhs=planes[:, t : t + 2, 0:HALF],
                    start=True,
                    stop=True,
                )

        def quantise_a(c, col0, ncols):
            cols = slice(col0, col0 + ncols)
            nc.vector.quantize_mx(
                out=quantised[c][0][:, cols].bitcast(E4M3X4),
                scales=quantised[c][1][:, cols],
                in_=grouped[c][0][:, PACK * col0 : PACK * (col0 + ncols)],
            )

        def quantise_g(c):
            nc.vector.quantize_mx(
                out=quantised[c][2][:].bitcast(E5M2X4), scales=quantised[c][3][:], in_=grouped[c][1][:]
            )

        def multiply(c, widths, first, last):
            a_codes, a_scales, g_codes, g_scales = quantised[c]
            for m, n in widths:
                cols = slice(m * P, (m + 1) * P)
                nc.tensor.matmul_mx(
                    out=acc[m][:, 0:n],
                    lhsT=a_codes[:, cols].bitcast(E4M3X4),
                    lhsT_scale=a_scales[:, cols],
                    rhs=g_codes[:, 0:n].bitcast(E5M2X4),
                    rhs_scale=g_scales[:, 0:n],
                    start=first,
                    stop=last,
                )

        for c in range(PASSES):
            new_tiles(c)
            a_grp, g_grp = grouped[c]
            if c + 2 in VIA_PE:
                pass_through(c + 2)
            if c == 0:
                for x_raw in (a_raw[0], g_raw[0]):
                    diag = x_raw[:].rearrange("p (t r) -> p t r", r=DIAG_PITCH)[:, :, 0:P]
                    nc.vector.tensor_tensor(
                        out=diag, in0=diag, in1=tri_bf[:].unsqueeze(1).to_broadcast([P, PACK, P]), op=ALU.mult
                    )
            if c == PASSES - 1:
                regroup(nc.scalar.copy, g_grp, g_raw[c], P, COLS - P)
                regroup(nc.scalar.copy, a_grp, a_raw[c], 0, HALF)
                regroup(nc.vector.tensor_copy, g_grp, g_raw[c], 0, P)
                regroup(nc.vector.tensor_copy, a_grp, a_raw[c], HALF, HALF)
                quantise_g(c)
                for m in (3, 2):
                    quantise_a(c, m * P, P)
                    multiply(c, ((m, COLS),), False, True)
                    nc.scalar.copy(out=out_sb[m][:, 0 : m * P], in_=acc[m][:, 0 : m * P])
                quantise_a(c, 0, HALF)
                multiply(c, ((1, COLS), (0, COLS)), False, True)
            else:
                if c in VIA_PE:
                    split = COLS - G_COLS_ON_SCALAR
                    regroup(nc.scalar.copy, a_grp, a_raw[c], HALF, HALF)
                    nc.scalar.copy(out=a_grp[:, 0 : PACK * HALF], in_=passed[c][:])
                    regroup(nc.scalar.copy, g_grp, g_raw[c], split, COLS - split)
                    regroup(nc.vector.tensor_copy, g_grp, g_raw[c], 0, split)
                else:
                    regroup(nc.scalar.copy, a_grp, a_raw[c], 0, COLS)
                    regroup(nc.vector.tensor_copy, g_grp, g_raw[c], 0, COLS)
                for b in range(c - (0 < c <= CATCH_UP), c + (c >= CATCH_UP)):
                    quantise_a(b, 0, COLS)
                    quantise_g(b)
                    multiply(b, [(m, COLS) for m in (3, 2, 1, 0)], b == 0, False)

        def store(m):
            nc.sync.dma_start(out=out[m * P : (m + 1) * P, 0 : (m + 1) * P], in_=out_sb[m][:])

        def mask_diagonal(m):
            block = slice(m * P, (m + 1) * P)
            nc.vector.tensor_tensor(out=out_sb[m][:, block], in0=acc[m][:, block], in1=tri_f32, op=ALU.mult)

        for m in (3, 2):
            nc.sync.dma_start(out=out[m * P : (m + 1) * P, 0 : m * P], in_=out_sb[m][:, 0 : m * P])
        for m in (3, 2):
            mask_diagonal(m)
            block = slice(m * P, (m + 1) * P)
            nc.sync.dma_start(out=out[block, block], in_=out_sb[m][:, block])
        nc.vector.tensor_tensor(out=out_sb[1][:], in0=acc[1][:, 0 : 2 * P], in1=out_mask[:], op=ALU.mult)
        store(1)
        mask_diagonal(0)
        store(0)
